import numpy as np
import ml_dtypes


def mxq(x, axis, fmt="e4m3"):
    dtype, down = {"e4m3": (ml_dtypes.float8_e4m3fn, 7), "e5m2": (ml_dtypes.float8_e5m2, 14)}[fmt]
    v = np.moveaxis(np.asarray(x, np.float32).astype(ml_dtypes.bfloat16).astype(np.float64), axis, -1)
    blocks = v.reshape(v.shape[:-1] + (-1, 32))
    amax = np.abs(blocks).max(-1, keepdims=True)
    byte = np.maximum(np.where(amax > 0, np.frexp(amax)[1] - 1 + 127, 0) - down, 1)
    scale = np.exp2(byte - 127.0)
    codes = (blocks / scale).astype(np.float32).astype(dtype).astype(np.float64)
    return np.moveaxis((codes * scale).reshape(v.shape), -1, axis)


WIDE = False


def mx_kscale(k):
    if not WIDE:
        return np.ones(k)
    levels = np.array([10, -10, 5, -5, 0])
    a = np.random.permutation(np.resize(levels, k // 512 * 4)).reshape(k // 512, 4)
    idx = np.arange(k)
    return np.exp2(a[idx // 512, idx % 128 // 32])


BF16 = ml_dtypes.bfloat16


def bf(x):
    return np.asarray(x, np.float32).astype(BF16)


def f64(x):
    return np.asarray(x).astype(np.float64)


B, N, E, H, G, C, EO = 16, 512, 256, 2, 128, 512, 1024
D = E // H
NB = N // C


def silu(v):
    return v / (1.0 + np.exp(-v))


def setup_inputs():
    s = mx_kscale(N)
    return {"q": bf(silu(0.4 * np.random.standard_normal((B, H, N, D)))),
            "k": bf(silu(0.4 * np.random.standard_normal((B, H, N, D))) * s[:, None]),
            "v": bf(silu(0.4 * np.random.standard_normal((B, H, N, D))) / s[:, None]),
            "log_slope": bf(-(3.0 + 5.0 * np.random.random(H)) / N)}


def reference(q, k, v, log_slope):
    ls = f64(log_slope)
    vq = mxq(f64(v), 2, "e4m3")
    idx = np.arange(N, dtype=np.float64)
    outs = []
    for i in range(NB):
        lo, hi = i * C, (i + 1) * C
        diff = idx[lo:hi, None] - idx[None, :hi]
        decay = np.where(diff >= 0, np.exp(ls[:, None, None] * np.maximum(diff, 0.0)), 0.0)
        energy = (f64(q)[:, :, lo:hi] @ f64(k)[:, :, :hi].transpose(0, 1, 3, 2)) * decay
        outs.append(mxq(energy, 3, "e4m3") @ vq[:, :, :hi])
    return np.concatenate(outs, axis=2)

@@ -1,0 +1,173 @@
+from contextlib import ExitStack
+
+import concourse.mybir as mybir
+from concourse.masks import make_identity
+
+BF16 = mybir.dt.bfloat16
+F32 = mybir.dt.float32
+I32 = mybir.dt.int32
+U32 = mybir.dt.uint32
+U8 = mybir.dt.uint8
+FP8X4 = mybir.dt.float8_e4m3fn_x4
+
+P = 128
+PACK = 4
+BATCHES = 16
+HEADS = 2
+SEQ = 512
+WIDTH = 128
+KEY_TILES = SEQ // P
+CLASSES = SEQ // P
+BANDS = SEQ // P
+BAND_ROWS = P // BANDS
+ALL_HEADS = BATCHES * HEADS
+
+FLOPS = 2 * 2 * ALL_HEADS * SEQ * SEQ * WIDTH
+
+
+def tile_tnlattention_pa_t_kernel(tc, q, k, v, log_slope, out):
+    nc = tc.nc
+    with ExitStack() as ctx:
+        const = ctx.enter_context(tc.tile_pool(name="const", bufs=1))
+        resident = ctx.enter_context(tc.tile_pool(name="resident", bufs=1))
+        work = ctx.enter_context(tc.tile_pool(name="work", bufs=3))
+        psum_t = ctx.enter_context(tc.psum_pool(name="psum_t", bufs=2))
+        psum_e = ctx.enter_context(tc.psum_pool(name="psum_e", bufs=4))
+        psum_o = ctx.enter_context(tc.psum_pool(name="psum_o", bufs=2))
+        ctx.enter_context(tc.manual_schedule())
+
+        slope_bf = const.tile([P, HEADS], BF16)
+        nc.scalar.dma_start(out=slope_bf[:], in_=log_slope.partition_broadcast(P))
+        q_sb, k_sb, v_sb = [], [], []
+        for b in range(BATCHES):
+            q_sb.append(resident.tile([P, HEADS, CLASSES, WIDTH], BF16, name="q%d" % b))
+            k_sb.append(resident.tile([P, HEADS, KEY_TILES, WIDTH], BF16, name="k%d" % b))
+            v_sb.append(resident.tile([P, HEADS, KEY_TILES, WIDTH], BF16, name="v%d" % b))
+            nc.sync.dma_start(out=q_sb[b][:], in_=q[b].rearrange("h (m c) d -> m h c d", c=CLASSES))
+            nc.sync.dma_start(out=k_sb[b][:], in_=k[b].rearrange("h (t p) d -> p h t d", p=P))
+            nc.sync.dma_start(out=v_sb[b][:], in_=v[b].rearrange("h (t p) d -> p h t d", p=P))
+
+        distance_int = const.tile([P, SEQ], I32)
+        nc.gpsimd.iota(
+            distance_int[:],
+            pattern=[[1, CLASSES], [PACK, BAND_ROWS], [-P, KEY_TILES]],
+            base=P * (BANDS - 1),
+            channel_multiplier=-1,
+        )
+        identity = const.tile([P, P], BF16)
+        make_identity(nc, identity[:])
+
+        slope = const.tile([P, HEADS], F32)
+        nc.vector.tensor_copy(out=slope[:], in_=slope_bf[:])
+        distance = const.tile([P, SEQ], F32)
+        nc.vector.tensor_copy(out=distance[:], in_=distance_int[:])
+        not_later = const.tile([P, SEQ], F32)
+        nc.vector.tensor_single_scalar(out=not_later[:], in_=distance[:], scalar=0.0, op=mybir.AluOpType.is_ge)
+        nc.vector.tensor_scalar_max(out=distance[:], in0=distance[:], scalar1=0.0)
+
+        decay = const.tile([P, HEADS, CLASSES, BAND_ROWS, KEY_TILES], F32)
+        grouped = []
+        for h in range(HEADS):
+            decay_h = decay[:, h, :, :, :].rearrange("p c r u -> p (c r u)")
+            nc.scalar.activation(
+                out=decay_h,
+                in_=distance[:],
+                func=mybir.ActivationFunctionType.Exp,
+                scale=slope[:, h : h + 1],
+            )
+            grouped.append(const.tile([P, CLASSES, P, PACK], BF16, name="grouped%d" % h, align_bytes=64))
+            nc.vector.memset(grouped[h][:], 0.0)
+            nc.vector.tensor_tensor(out=decay_h, in0=decay_h, in1=not_later[:], op=mybir.AluOpType.mult)
+
+        qk_t = {}
+        e_words, e_scales = {}, {}
+        v_grouped, v_words, v_scales = {}, {}, {}
+
+        def transpose_q_k(head):
+            b, h = divmod(head, HEADS)
+            flipped = psum_t.tile([P, 2, PACK, P], BF16)
+            for c in range(CLASSES):
+                nc.tensor.transpose(flipped[:, 0, c, :], q_sb[b][:, h, c, :], identity[:])
+            for t in range(KEY_TILES):
+                nc.tensor.transpose(flipped[:, 1, t, :], k_sb[b][:, h, t, :], identity[:])
+            qk_t[head] = work.tile([P, 2, PACK, P], BF16, name="qk_t")
+            nc.scalar.copy(out=qk_t[head][:], in_=flipped[:])
+
+        def regroup_v(b):
+            v_grouped[b] = work.tile([P, HEADS, WIDTH, PACK], BF16, name="v_grouped", align_bytes=64)
+            nc.scalar.copy(out=v_grouped[b][:], in_=v_sb[b][:].rearrange("p h t d -> p h d t"))
+
+        def quantise_v(b):
+            v_words[b] = work.tile([P, HEADS * WIDTH], U32, name="v_words", align_bytes=64)
+            v_scales[b] = work.tile([P, HEADS * WIDTH], U8, name="v_scales", align_bytes=64)
+            nc.vector.quantize_mx(
+                out=v_words[b][:].bitcast(FP8X4),
+                scales=v_scales[b][:],
+                in_=v_grouped[b][:].rearrange("p h d t -> p (h d t)"),
+            )
+
+        def energy_of_band(head, s):
+            h = head % HEADS
+            rows = slice(s * BAND_ROWS, (s + 1) * BAND_ROWS)
+            product = psum_e.tile([P, KEY_TILES, CLASSES, BAND_ROWS], F32)
+            for t in range(s + 1):
+                nc.tensor.matmul(
+                    out=product[:, t, :, :],
+                    lhsT=qk_t[head][:, 1, t, :],
+                    rhs=qk_t[head][:, 0, :, rows],
+                    start=True,
+                    stop=True,
+                )
+            nc.vector.tensor_tensor(
+                out=grouped[head % HEADS][:, :, rows, 0 : s + 1],
+                in0=product[:, 0 : s + 1, :, :].rearrange("p t c r -> p c r t"),
+                in1=decay[:, h, :, :, KEY_TILES - 1 - s : KEY_TILES],
+                op=mybir.AluOpType.mult,
+            )
+
+        def quantise_energy(head):
+            e_words[head] = work.tile([P, SEQ], U32, name="e_words", align_bytes=64)
+            e_scales[head] = work.tile([P, SEQ], U8, name="e_scales", align_bytes=64)
+            nc.vector.quantize_mx(
+                out=e_words[head][:].bitcast(FP8X4),
+                scales=e_scales[head][:],
+                in_=grouped[head % HEADS][:].rearrange("p c m t -> p (c m t)"),
+            )
+
+        def output(head):
+            b, h = divmod(head, HEADS)
+            columns = slice(h * WIDTH, (h + 1) * WIDTH)
+            result = psum_o.tile([P, CLASSES, WIDTH], F32)
+            for c in range(CLASSES):
+                queries = slice(c * P, (c + 1) * P)
+                nc.tensor.matmul_mx(
+                    out=result[:, c, :],
+                    lhsT=e_words[head][:, queries].bitcast(FP8X4),
+                    lhsT_scale=e_scales[head][:, queries],
+                    rhs=v_words[b][:, columns].bitcast(FP8X4),
+                    rhs_scale=v_scales[b][:, columns],
+                    start=True,
+                    stop=True,
+                )
+            out_sb = resident.tile([P, CLASSES, WIDTH], F32, name="out%d" % head)
+            nc.scalar.copy(out=out_sb[:], in_=result[:])
+            nc.sync.dma_start(out=out[b, h].rearrange("(m c) d -> m c d", c=CLASSES), in_=out_sb[:])
+
+        for step in range(ALL_HEADS + 2):
+            if step < ALL_HEADS:
+                transpose_q_k(step)
+                if step % HEADS == 0:
+                    regroup_v(step // HEADS)
+            has_energy = 1 <= step <= ALL_HEADS
+            if has_energy:
+                energy_of_band(step - 1, 0)
+            if step >= 2:
+                quantise_energy(step - 2)
+            if has_energy:
+                energy_of_band(step - 1, 1)
+                if step % HEADS == 1:
+                    quantise_v(step // HEADS)
+                energy_of_band(step - 1, 2)
+                energy_of_band(step - 1, 3)
+            if step >= 2:
+                output(step - 2)

@@ -21,6 +21,7 @@ CLASSES = SEQ // P
 BANDS = SEQ // P
 BAND_ROWS = P // BANDS
 ALL_HEADS = BATCHES * HEADS
+GPSIMD_BANDS = 2
 
 FLOPS = 2 * 2 * ALL_HEADS * SEQ * SEQ * WIDTH
 
@@ -118,9 +119,15 @@ def tile_tnlattention_pa_t_kernel(tc, q, k, v, log_slope, out):
                     start=True,
                     stop=True,
                 )
-            nc.vector.tensor_tensor(
+            if s < GPSIMD_BANDS:
+                product_sb = work.tile([P, GPSIMD_BANDS, CLASSES, BAND_ROWS], F32, name="product_sb")
+                nc.scalar.copy(out=product_sb[:, 0 : s + 1, :, :], in_=product[:, 0 : s + 1, :, :])
+                multiplier, source = nc.gpsimd, product_sb
+            else:
+                multiplier, source = nc.vector, product
+            multiplier.tensor_tensor(
                 out=grouped[head % HEADS][:, :, rows, 0 : s + 1],
-                in0=product[:, 0 : s + 1, :, :].rearrange("p t c r -> p c r t"),
+                in0=source[:, 0 : s + 1, :, :].rearrange("p t c r -> p c r t"),
                 in1=decay[:, h, :, :, KEY_TILES - 1 - s : KEY_TILES],
                 op=mybir.AluOpType.mult,
             )
@@ -154,20 +161,21 @@ def tile_tnlattention_pa_t_kernel(tc, q, k, v, log_slope, out):
             nc.sync.dma_start(out=out[b, h].rearrange("(m c) d -> m c d", c=CLASSES), in_=out_sb[:])
 
         for step in range(ALL_HEADS + 2):
+            has_energy = 1 <= step <= ALL_HEADS
             if step < ALL_HEADS:
                 transpose_q_k(step)
-                if step % HEADS == 0:
-                    regroup_v(step // HEADS)
-            has_energy = 1 <= step <= ALL_HEADS
             if has_energy:
                 energy_of_band(step - 1, 0)
+                energy_of_band(step - 1, 1)
+            if step < ALL_HEADS and step % HEADS == 0:
+                regroup_v(step // HEADS)
+            if has_energy:
+                energy_of_band(step - 1, 2)
             if step >= 2:
                 quantise_energy(step - 2)
             if has_energy:
-                energy_of_band(step - 1, 1)
+                energy_of_band(step - 1, 3)
                 if step % HEADS == 1:
                     quantise_v(step // HEADS)
-                energy_of_band(step - 1, 2)
-                energy_of_band(step - 1, 3)
             if step >= 2:
                 output(step - 2)

@@ -21,7 +21,6 @@ CLASSES = SEQ // P
 BANDS = SEQ // P
 BAND_ROWS = P // BANDS
 ALL_HEADS = BATCHES * HEADS
-GPSIMD_BANDS = 2
 
 FLOPS = 2 * 2 * ALL_HEADS * SEQ * SEQ * WIDTH
 
@@ -119,18 +118,20 @@ def tile_tnlattention_pa_t_kernel(tc, q, k, v, log_slope, out):
                     start=True,
                     stop=True,
                 )
-            if s < GPSIMD_BANDS:
-                product_sb = work.tile([P, GPSIMD_BANDS, CLASSES, BAND_ROWS], F32, name="product_sb")
-                nc.scalar.copy(out=product_sb[:, 0 : s + 1, :, :], in_=product[:, 0 : s + 1, :, :])
-                multiplier, source = nc.gpsimd, product_sb
+            places = grouped[head % HEADS][:, :, rows, 0 : s + 1]
+            if s == 0:
+                dense = work.tile([P, CLASSES, BAND_ROWS, 1], BF16, name="dense")
+                target = dense[:]
             else:
-                multiplier, source = nc.vector, product
-            multiplier.tensor_tensor(
-                out=grouped[head % HEADS][:, :, rows, 0 : s + 1],
-                in0=source[:, 0 : s + 1, :, :].rearrange("p t c r -> p c r t"),
+                target = places
+            nc.vector.tensor_tensor(
+                out=target,
+                in0=product[:, 0 : s + 1, :, :].rearrange("p t c r -> p c r t"),
                 in1=decay[:, h, :, :, KEY_TILES - 1 - s : KEY_TILES],
                 op=mybir.AluOpType.mult,
             )
+            if s == 0:
+                nc.scalar.copy(out=places, in_=dense[:])
 
         def quantise_energy(head):
             e_words[head] = work.tile([P, SEQ], U32, name="e_words", align_bytes=64)
@@ -161,21 +162,20 @@ def tile_tnlattention_pa_t_kernel(tc, q, k, v, log_slope, out):
             nc.sync.dma_start(out=out[b, h].rearrange("(m c) d -> m c d", c=CLASSES), in_=out_sb[:])
 
         for step in range(ALL_HEADS + 2):
-            has_energy = 1 <= step <= ALL_HEADS
             if step < ALL_HEADS:
                 transpose_q_k(step)
+                if step % HEADS == 0:
+                    regroup_v(step // HEADS)
+            has_energy = 1 <= step <= ALL_HEADS
             if has_energy:
                 energy_of_band(step - 1, 0)
-                energy_of_band(step - 1, 1)
-            if step < ALL_HEADS and step % HEADS == 0:
-                regroup_v(step // HEADS)
-            if has_energy:
-                energy_of_band(step - 1, 2)
             if step >= 2:
                 quantise_energy(step - 2)
             if has_energy:
-                energy_of_band(step - 1, 3)
+                energy_of_band(step - 1, 1)
                 if step % HEADS == 1:
                     quantise_v(step // HEADS)
+                energy_of_band(step - 1, 2)
+                energy_of_band(step - 1, 3)
             if step >= 2:
                 output(step - 2)

@@ -161,7 +161,9 @@ def tile_tnlattention_pa_t_kernel(tc, q, k, v, log_slope, out):
             nc.scalar.copy(out=out_sb[:], in_=result[:])
             nc.sync.dma_start(out=out[b, h].rearrange("(m c) d -> m c d", c=CLASSES), in_=out_sb[:])
 
-        for step in range(ALL_HEADS + 2):
+        for step in range(ALL_HEADS + 3):
+            if step >= 3:
+                output(step - 3)
             if step < ALL_HEADS:
                 transpose_q_k(step)
                 if step % HEADS == 0:
@@ -169,7 +171,7 @@ def tile_tnlattention_pa_t_kernel(tc, q, k, v, log_slope, out):
             has_energy = 1 <= step <= ALL_HEADS
             if has_energy:
                 energy_of_band(step - 1, 0)
-            if step >= 2:
+            if 2 <= step <= ALL_HEADS + 1:
                 quantise_energy(step - 2)
             if has_energy:
                 energy_of_band(step - 1, 1)
@@ -177,5 +179,3 @@ def tile_tnlattention_pa_t_kernel(tc, q, k, v, log_slope, out):
                     quantise_v(step // HEADS)
                 energy_of_band(step - 1, 2)
                 energy_of_band(step - 1, 3)
-            if step >= 2:
-                output(step - 2)

from contextlib import ExitStack

import concourse.mybir as mybir
from concourse.masks import make_identity

BF16 = mybir.dt.bfloat16
F32 = mybir.dt.float32
I32 = mybir.dt.int32
U32 = mybir.dt.uint32
U8 = mybir.dt.uint8
FP8X4 = mybir.dt.float8_e4m3fn_x4

P = 128
PACK = 4
BATCHES = 16
HEADS = 2
SEQ = 512
WIDTH = 128
KEY_TILES = SEQ // P
CLASSES = SEQ // P
BANDS = SEQ // P
BAND_ROWS = P // BANDS
ALL_HEADS = BATCHES * HEADS

FLOPS = 2 * 2 * ALL_HEADS * SEQ * SEQ * WIDTH


def tile_tnlattention_pa_t_kernel(tc, q, k, v, log_slope, out):
    nc = tc.nc
    with ExitStack() as ctx:
        const = ctx.enter_context(tc.tile_pool(name="const", bufs=1))
        resident = ctx.enter_context(tc.tile_pool(name="resident", bufs=1))
        work = ctx.enter_context(tc.tile_pool(name="work", bufs=3))
        psum_t = ctx.enter_context(tc.psum_pool(name="psum_t", bufs=2))
        psum_e = ctx.enter_context(tc.psum_pool(name="psum_e", bufs=4))
        psum_o = ctx.enter_context(tc.psum_pool(name="psum_o", bufs=2))
        ctx.enter_context(tc.manual_schedule())

        slope_bf = const.tile([P, HEADS], BF16)
        nc.scalar.dma_start(out=slope_bf[:], in_=log_slope.partition_broadcast(P))
        q_sb, k_sb, v_sb = [], [], []
        for b in range(BATCHES):
            q_sb.append(resident.tile([P, HEADS, CLASSES, WIDTH], BF16, name="q%d" % b))
            k_sb.append(resident.tile([P, HEADS, KEY_TILES, WIDTH], BF16, name="k%d" % b))
            v_sb.append(resident.tile([P, HEADS, KEY_TILES, WIDTH], BF16, name="v%d" % b))
            nc.sync.dma_start(out=q_sb[b][:], in_=q[b].rearrange("h (m c) d -> m h c d", c=CLASSES))
            nc.sync.dma_start(out=k_sb[b][:], in_=k[b].rearrange("h (t p) d -> p h t d", p=P))
            nc.sync.dma_start(out=v_sb[b][:], in_=v[b].rearrange("h (t p) d -> p h t d", p=P))

        distance_int = const.tile([P, SEQ], I32)
        nc.gpsimd.iota(
            distance_int[:],
            pattern=[[1, CLASSES], [PACK, BAND_ROWS], [-P, KEY_TILES]],
            base=P * (BANDS - 1),
            channel_multiplier=-1,
        )
        identity = const.tile([P, P], BF16)
        make_identity(nc, identity[:])

        slope = const.tile([P, HEADS], F32)
        nc.vector.tensor_copy(out=slope[:], in_=slope_bf[:])
        distance = const.tile([P, SEQ], F32)
        nc.vector.tensor_copy(out=distance[:], in_=distance_int[:])
        not_later = const.tile([P, SEQ], F32)
        nc.vector.tensor_single_scalar(out=not_later[:], in_=distance[:], scalar=0.0, op=mybir.AluOpType.is_ge)
        nc.vector.tensor_scalar_max(out=distance[:], in0=distance[:], scalar1=0.0)

        decay = const.tile([P, HEADS, CLASSES, BAND_ROWS, KEY_TILES], F32)
        grouped = []
        for h in range(HEADS):
            decay_h = decay[:, h, :, :, :].rearrange("p c r u -> p (c r u)")
            nc.scalar.activation(
                out=decay_h,
                in_=distance[:],
                func=mybir.ActivationFunctionType.Exp,
                scale=slope[:, h : h + 1],
            )
            grouped.append(const.tile([P, CLASSES, P, PACK], BF16, name="grouped%d" % h, align_bytes=64))
            nc.vector.memset(grouped[h][:], 0.0)
            nc.vector.tensor_tensor(out=decay_h, in0=decay_h, in1=not_later[:], op=mybir.AluOpType.mult)

        qk_t = {}
        e_words, e_scales = {}, {}
        v_grouped, v_words, v_scales = {}, {}, {}

        def transpose_q_k(head):
            b, h = divmod(head, HEADS)
            flipped = psum_t.tile([P, 2, PACK, P], BF16)
            for c in range(CLASSES):
                nc.tensor.transpose(flipped[:, 0, c, :], q_sb[b][:, h, c, :], identity[:])
            for t in range(KEY_TILES):
                nc.tensor.transpose(flipped[:, 1, t, :], k_sb[b][:, h, t, :], identity[:])
            qk_t[head] = work.tile([P, 2, PACK, P], BF16, name="qk_t")
            nc.scalar.copy(out=qk_t[head][:], in_=flipped[:])

        def regroup_v(b):
            v_grouped[b] = work.tile([P, HEADS, WIDTH, PACK], BF16, name="v_grouped", align_bytes=64)
            nc.scalar.copy(out=v_grouped[b][:], in_=v_sb[b][:].rearrange("p h t d -> p h d t"))

        def quantise_v(b):
            v_words[b] = work.tile([P, HEADS * WIDTH], U32, name="v_words", align_bytes=64)
            v_scales[b] = work.tile([P, HEADS * WIDTH], U8, name="v_scales", align_bytes=64)
            nc.vector.quantize_mx(
                out=v_words[b][:].bitcast(FP8X4),
                scales=v_scales[b][:],
                in_=v_grouped[b][:].rearrange("p h d t -> p (h d t)"),
            )

        def energy_of_band(head, s):
            h = head % HEADS
            rows = slice(s * BAND_ROWS, (s + 1) * BAND_ROWS)
            product = psum_e.tile([P, KEY_TILES, CLASSES, BAND_ROWS], F32)
            for t in range(s + 1):
                nc.tensor.matmul(
                    out=product[:, t, :, :],
                    lhsT=qk_t[head][:, 1, t, :],
                    rhs=qk_t[head][:, 0, :, rows],
                    start=True,
                    stop=True,
                )
            places = grouped[head % HEADS][:, :, rows, 0 : s + 1]
            if s == 0:
                dense = work.tile([P, CLASSES, BAND_ROWS, 1], BF16, name="dense")
                target = dense[:]
            else:
                target = places
            nc.vector.tensor_tensor(
                out=target,
                in0=product[:, 0 : s + 1, :, :].rearrange("p t c r -> p c r t"),
                in1=decay[:, h, :, :, KEY_TILES - 1 - s : KEY_TILES],
                op=mybir.AluOpType.mult,
            )
            if s == 0:
                nc.scalar.copy(out=places, in_=dense[:])

        def quantise_energy(head):
            e_words[head] = work.tile([P, SEQ], U32, name="e_words", align_bytes=64)
            e_scales[head] = work.tile([P, SEQ], U8, name="e_scales", align_bytes=64)
            nc.vector.quantize_mx(
                out=e_words[head][:].bitcast(FP8X4),
                scales=e_scales[head][:],
                in_=grouped[head % HEADS][:].rearrange("p c m t -> p (c m t)"),
            )

        def output(head):
            b, h = divmod(head, HEADS)
            columns = slice(h * WIDTH, (h + 1) * WIDTH)
            result = psum_o.tile([P, CLASSES, WIDTH], F32)
            for c in range(CLASSES):
                queries = slice(c * P, (c + 1) * P)
                nc.tensor.matmul_mx(
                    out=result[:, c, :],
                    lhsT=e_words[head][:, queries].bitcast(FP8X4),
                    lhsT_scale=e_scales[head][:, queries],
                    rhs=v_words[b][:, columns].bitcast(FP8X4),
                    rhs_scale=v_scales[b][:, columns],
                    start=True,
                    stop=True,
                )
            out_sb = resident.tile([P, CLASSES, WIDTH], F32, name="out%d" % head)
            nc.scalar.copy(out=out_sb[:], in_=result[:])
            nc.sync.dma_start(out=out[b, h].rearrange("(m c) d -> m c d", c=CLASSES), in_=out_sb[:])

        for step in range(ALL_HEADS + 3):
            if step >= 3:
                output(step - 3)
            if step < ALL_HEADS:
                transpose_q_k(step)
                if step % HEADS == 0:
                    regroup_v(step // HEADS)
            has_energy = 1 <= step <= ALL_HEADS
            if has_energy:
                energy_of_band(step - 1, 0)
            if 2 <= step <= ALL_HEADS + 1:
                quantise_energy(step - 2)
            if has_energy:
                energy_of_band(step - 1, 1)
                if step % HEADS == 1:
                    quantise_v(step // HEADS)
                energy_of_band(step - 1, 2)
                energy_of_band(step - 1, 3)
